import numpy as np
import ml_dtypes


def mxq(x, axis, fmt="e4m3"):
    dtype, down = {"e4m3": (ml_dtypes.float8_e4m3fn, 7), "e5m2": (ml_dtypes.float8_e5m2, 14)}[fmt]
    v = np.moveaxis(np.asarray(x, np.float32).astype(ml_dtypes.bfloat16).astype(np.float64), axis, -1)
    blocks = v.reshape(v.shape[:-1] + (-1, 32))
    amax = np.abs(blocks).max(-1, keepdims=True)
    byte = np.maximum(np.where(amax > 0, np.frexp(amax)[1] - 1 + 127, 0) - down, 1)
    scale = np.exp2(byte - 127.0)
    codes = (blocks / scale).astype(np.float32).astype(dtype).astype(np.float64)
    return np.moveaxis((codes * scale).reshape(v.shape), -1, axis)


WIDE = False


def mx_kscale(k):
    if not WIDE:
        return np.ones(k)
    levels = np.array([10, -10, 5, -5, 0])
    a = np.random.permutation(np.resize(levels, k // 512 * 4)).reshape(k // 512, 4)
    idx = np.arange(k)
    return np.exp2(a[idx // 512, idx % 128 // 32])


BF16 = ml_dtypes.bfloat16


def bf(x):
    return np.asarray(x, np.float32).astype(BF16)


def f64(x):
    return np.asarray(x).astype(np.float64)


E2M1 = np.array([0.0, 0.5, 1.0, 1.5, 2.0, 3.0, 4.0, 6.0, -0.0, -0.5, -1.0, -1.5, -2.0, -3.0, -4.0, -6.0])


def pack_weight(w, fmt):
    k, n = w.shape
    w = f64(bf(w)).reshape(k // 32, 32, n)
    amax = np.abs(w).max(1)
    if fmt == "e4m3":
        byte = np.frexp(amax)[1] - 1 + 127 - 7
    else:
        mant, ex = np.frexp(amax / 6.0)
        byte = np.where(mant > 0.5, ex, ex - 1) + 127
    byte = np.clip(np.where(amax > 0, byte, 1), 1, 254)
    scaled = (w * np.exp2(127.0 - byte)[:, None, :]).reshape(k, n).astype(np.float32)
    by_word = np.ascontiguousarray(scaled.reshape(k // 512, 128, 4, n).transpose(0, 1, 3, 2))
    if fmt == "e4m3":
        words = by_word.astype(ml_dtypes.float8_e4m3fn).view(np.uint8)
    else:
        c = by_word.astype(ml_dtypes.float4_e2m1fn).view(np.uint8) & 0xF
        words = c[..., 0::2] | (c[..., 1::2] << 4)
    return np.ascontiguousarray(words), np.ascontiguousarray(byte.astype(np.uint8).reshape(k // 512, 16, n))


def unpack_weight(words, scales, fmt):
    g, p, n, _ = words.shape
    if fmt == "e4m3":
        vals = np.ascontiguousarray(words).view(ml_dtypes.float8_e4m3fn).astype(np.float64)
    else:
        nib = np.empty((g, p, n, 4), np.uint8)
        nib[..., 0::2] = words & 0xF
        nib[..., 1::2] = words >> 4
        vals = E2M1[nib]
    vals = vals * np.repeat(np.exp2(scales.astype(np.float64) - 127.0), 8, axis=1)[..., None]
    return vals.transpose(0, 1, 3, 2).reshape(g * 512, n)


B, F, G, N, L = 256, 512, 16, 100, 7
S2 = (L + 1) ** 2


def setup_inputs():
    s = mx_kscale(F)
    x = bf(np.random.standard_normal((B, F, S2)) * s[None, :, None])
    psi = np.random.standard_normal((G, F, S2)) / s[None, :, None]
    words, scales = pack_weight(psi.reshape(-1, S2), "e4m3")
    return {"x": x, "psi_words": words, "psi_scales": scales}


def reference(x, psi_words, psi_scales):
    xq = mxq(f64(x), 1, "e4m3")
    pq = unpack_weight(psi_words, psi_scales, "e4m3").reshape(G, F, S2)
    scale = 1.0 / np.sqrt(F)
    outs = []
    for l in range(L + 1):
        s, d = l * l, 2 * l + 1
        a = xq[:, :, s:s + d].transpose(0, 2, 1).reshape(B * d, F)
        p = pq[:, :, s:s + d].transpose(1, 0, 2).reshape(F, G * d)
        o = scale * (a @ p)
        outs.append(o.reshape(B, d, G, d).transpose(2, 0, 1, 3).reshape(G, B, d * d))
    return np.concatenate(outs, axis=-1)

@@ -1,0 +1,216 @@
+from contextlib import ExitStack
+import math
+
+import concourse.mybir as mybir
+
+BF16 = mybir.dt.bfloat16
+F32 = mybir.dt.float32
+I32 = mybir.dt.int32
+U32 = mybir.dt.uint32
+U8 = mybir.dt.uint8
+FP8X4 = mybir.dt.float8_e4m3fn_x4
+
+P = 128
+PACK = 4
+BATCH = 256
+FEATURES = P * PACK
+COEFFS = 64
+DEGREES = 8
+OUT_FEATURES = 16
+ROW = 680
+SCALE = 1.0 / math.sqrt(FEATURES)
+
+assert ROW == sum((2 * degree + 1) ** 2 for degree in range(DEGREES))
+
+FLOPS = 2 * FEATURES * BATCH * OUT_FEATURES * ROW
+
+HALVES = BATCH // P
+CHUNK_ROWS = 16
+CHUNKS = P // CHUNK_ROWS
+RAW_BUFFERS = 6
+
+SCALAR_COEFFS = COEFFS // 4
+VECTOR_COEFFS = COEFFS - SCALAR_COEFFS
+RUN = 4
+QUANT_COEFFS = 8
+
+PASS_COLS = 128
+GROUP_FEATURES = 8
+GROUPS = OUT_FEATURES // GROUP_FEATURES
+PASSES_PER_BANK = 4
+PSUM_BANKS = 8
+ROW_BUFFERS = 3
+STORE_FEATURES = 4
+
+
+def window(degree):
+    first = degree * degree
+    beyond = first + 2 * degree + 1
+    start = first - first % PACK
+    stop = beyond + (-beyond) % PACK
+    return start, stop - start
+
+
+def banks_of_a_half():
+    banks = []
+    for group in range(GROUPS):
+        for degree in reversed(range(DEGREES)):
+            for first_u in reversed(range(0, 2 * degree + 1, PASSES_PER_BANK)):
+                banks.append((group, degree, first_u))
+    return banks
+
+
+def tile_s2conv_pa_t_e_kernel(tc, x, psi_words, psi_scales, out):
+    nc = tc.nc
+    banks = banks_of_a_half()
+    banks_per_chunk = len(banks) // CHUNKS
+    assert banks_per_chunk * CHUNKS == len(banks)
+
+    with ExitStack() as ctx:
+        const = ctx.enter_context(tc.tile_pool(name="const", bufs=1))
+        keep = ctx.enter_context(tc.tile_pool(name="keep", bufs=1))
+        stream = ctx.enter_context(tc.tile_pool(name="stream", bufs=RAW_BUFFERS))
+        outs = ctx.enter_context(tc.tile_pool(name="outs", bufs=ROW_BUFFERS))
+        psum = ctx.enter_context(tc.psum_pool(name="psum", bufs=PSUM_BANKS))
+        ctx.enter_context(tc.manual_schedule())
+
+        psi_raw = const.tile([P, OUT_FEATURES, COEFFS], U32)
+        nc.sync.dma_start(
+            out=psi_raw[:].bitcast(I32),
+            in_=psi_words.rearrange("g p n t -> p g (n t)").bitcast(I32),
+        )
+        scale_raw = const.tile([P, OUT_FEATURES, COEFFS], U8)
+        nc.vector.memset(scale_raw[:].bitcast(I32), 0)
+        for quadrant in range(4):
+            nc.sync.dma_start(
+                out=scale_raw[32 * quadrant : 32 * quadrant + 4, :, :].bitcast(I32),
+                in_=psi_scales[:, 4 * quadrant : 4 * quadrant + 4, :]
+                .rearrange("g r n -> r g n")
+                .bitcast(I32),
+            )
+        filter_codes = const.tile([P, DEGREES, GROUPS, PASS_COLS], U32, align_bytes=64)
+        filter_scales = const.tile([P, DEGREES, GROUPS, PASS_COLS], U8, align_bytes=64)
+        nc.vector.memset(filter_codes[:].bitcast(I32), 0)
+        nc.vector.memset(filter_scales[:].bitcast(I32), 0)
+        for degree in range(DEGREES):
+            start, width = window(degree)
+            used = GROUP_FEATURES * width
+            nc.vector.tensor_copy(
+                out=filter_codes[:, degree, :, 0:used]
+                .bitcast(I32)
+                .rearrange("p h (g w) -> p h g w", w=width),
+                in_=psi_raw[:, :, start : start + width]
+                .bitcast(I32)
+                .rearrange("p (h g) w -> p h g w", g=GROUP_FEATURES),
+            )
+            nc.vector.tensor_copy(
+                out=filter_scales[:, degree, :, 0:used]
+                .bitcast(I32)
+                .rearrange("p h (g w) -> p h g w", w=width // 4),
+                in_=scale_raw[:, :, start : start + width]
+                .bitcast(I32)
+                .rearrange("p (h g) w -> p h g w", g=GROUP_FEATURES),
+            )
+
+        grouped_vector = keep.tile([P, VECTOR_COEFFS, P * PACK], BF16, align_bytes=64)
+        grouped_scalar = keep.tile([P, SCALAR_COEFFS, P * PACK], BF16, align_bytes=64)
+        x_codes = keep.tile([P, COEFFS, P], U32, align_bytes=64)
+        x_scales = keep.tile([P, COEFFS, P], U8, align_bytes=64)
+        x_rows = x.rearrange("b (p j) n -> p b (j n)", j=PACK)
+        row_tiles = {}
+
+        def load_chunk(half, chunk):
+            first_row = half * P + chunk * CHUNK_ROWS
+            raw = stream.tile([P, CHUNK_ROWS * PACK, COEFFS], BF16)
+            nc.sync.dma_start(
+                out=raw[:].rearrange("p (b j) n -> p b (j n)", j=PACK),
+                in_=x_rows[:, first_row : first_row + CHUNK_ROWS, :],
+            )
+            return raw
+
+        def regroup_chunk(raw, chunk):
+            cols = slice(chunk * CHUNK_ROWS * PACK, (chunk + 1) * CHUNK_ROWS * PACK)
+            nc.vector.tensor_copy(
+                out=grouped_vector[:, :, cols].rearrange("p (c i) r -> p c r i", i=RUN),
+                in_=raw[:, :, 0:VECTOR_COEFFS].rearrange("p r (c i) -> p c r i", i=RUN),
+            )
+            nc.scalar.copy(
+                out=grouped_scalar[:, :, cols].rearrange("p (c i) r -> p c r i", i=RUN),
+                in_=raw[:, :, VECTOR_COEFFS:COEFFS].rearrange("p r (c i) -> p c r i", i=RUN),
+            )
+
+        def quantise_half():
+            for first_n in reversed(range(0, COEFFS, QUANT_COEFFS)):
+                if first_n >= VECTOR_COEFFS:
+                    source = grouped_scalar[:, first_n - VECTOR_COEFFS :, :]
+                else:
+                    source = grouped_vector[:, first_n:, :]
+                coeffs = slice(first_n, first_n + QUANT_COEFFS)
+                nc.vector.quantize_mx(
+                    out=x_codes[:, coeffs, :].rearrange("p n b -> p (n b)").bitcast(FP8X4),
+                    scales=x_scales[:, coeffs, :].rearrange("p n b -> p (n b)"),
+                    in_=source[:, 0:QUANT_COEFFS, :].rearrange("p n r -> p (n r)"),
+                )
+
+        def multiply_bank(half, group, degree, first_u):
+            if (half, group) not in row_tiles:
+                rows = outs.tile([P, GROUP_FEATURES, ROW], F32)
+                row_tiles[(half, group)] = rows
+            rows = row_tiles[(half, group)]
+            size = 2 * degree + 1
+            first_n = degree * degree
+            block = sum((2 * k + 1) ** 2 for k in range(degree))
+            start, width = window(degree)
+            count = min(PASSES_PER_BANK, size - first_u)
+            bank = psum.tile([P, PASSES_PER_BANK, PASS_COLS], F32)
+            for k in range(count):
+                n = first_n + first_u + k
+                nc.tensor.matmul_mx(
+                    out=bank[:, k, :],
+                    lhsT=x_codes[:, n, :].bitcast(FP8X4),
+                    lhsT_scale=x_scales[:, n, :],
+                    rhs=filter_codes[:, degree, group, :].bitcast(FP8X4),
+                    rhs_scale=filter_scales[:, degree, group, :],
+                    start=True,
+                    stop=True,
+                )
+            skip = first_n - start
+            products = bank[:, 0:count, 0 : GROUP_FEATURES * width].rearrange(
+                "p k (g w) -> p g k w", w=width
+            )
+            place = block + first_u * size
+            nc.scalar.mul(
+                out=rows[:, :, place : place + count * size].rearrange(
+                    "p g (k m) -> p g k m", m=size
+                ),
+                in_=products[:, :, :, skip : skip + size],
+                mul=SCALE,
+            )
+
+        def store_half(half):
+            for group in range(GROUPS):
+                rows = row_tiles[(half, group)]
+                for first_g in range(0, GROUP_FEATURES, STORE_FEATURES):
+                    g = group * GROUP_FEATURES + first_g
+                    nc.sync.dma_start(
+                        out=out[g : g + STORE_FEATURES, half * P : (half + 1) * P, :].rearrange(
+                            "g b c -> b g c"
+                        ),
+                        in_=rows[:, first_g : first_g + STORE_FEATURES, :],
+                    )
+
+        for step in range(HALVES + 1):
+            for chunk in range(CHUNKS):
+                if step < HALVES:
+                    raw = load_chunk(step, chunk)
+                if step > 0:
+                    for group, degree, first_u in banks[
+                        chunk * banks_per_chunk : (chunk + 1) * banks_per_chunk
+                    ]:
+                        multiply_bank(step - 1, group, degree, first_u)
+                if step < HALVES:
+                    regroup_chunk(raw, chunk)
+            if step > 0:
+                store_half(step - 1)
+            if step < HALVES:
+                quantise_half()

@@ -27,12 +27,13 @@ FLOPS = 2 * FEATURES * BATCH * OUT_FEATURES * ROW
 HALVES = BATCH // P
 CHUNK_ROWS = 16
 CHUNKS = P // CHUNK_ROWS
-RAW_BUFFERS = 6
+RAW_BUFFERS = 5
 
 SCALAR_COEFFS = COEFFS // 4
 VECTOR_COEFFS = COEFFS - SCALAR_COEFFS
 RUN = 4
-QUANT_COEFFS = 8
+QUANT_ROWS = 64
+CHUNKS_PER_QUANT = QUANT_ROWS // CHUNK_ROWS
 
 PASS_COLS = 128
 GROUP_FEATURES = 8
@@ -70,6 +71,7 @@ def tile_s2conv_pa_t_e_kernel(tc, x, psi_words, psi_scales, out):
         const = ctx.enter_context(tc.tile_pool(name="const", bufs=1))
         keep = ctx.enter_context(tc.tile_pool(name="keep", bufs=1))
         stream = ctx.enter_context(tc.tile_pool(name="stream", bufs=RAW_BUFFERS))
+        words = ctx.enter_context(tc.tile_pool(name="words", bufs=HALVES))
         outs = ctx.enter_context(tc.tile_pool(name="outs", bufs=ROW_BUFFERS))
         psum = ctx.enter_context(tc.psum_pool(name="psum", bufs=PSUM_BANKS))
         ctx.enter_context(tc.manual_schedule())
@@ -112,11 +114,10 @@ def tile_s2conv_pa_t_e_kernel(tc, x, psi_words, psi_scales, out):
                 .rearrange("p (h g) w -> p h g w", g=GROUP_FEATURES),
             )
 
-        grouped_vector = keep.tile([P, VECTOR_COEFFS, P * PACK], BF16, align_bytes=64)
-        grouped_scalar = keep.tile([P, SCALAR_COEFFS, P * PACK], BF16, align_bytes=64)
-        x_codes = keep.tile([P, COEFFS, P], U32, align_bytes=64)
-        x_scales = keep.tile([P, COEFFS, P], U8, align_bytes=64)
+        grouped_vector = keep.tile([P, VECTOR_COEFFS, QUANT_ROWS * PACK], BF16, align_bytes=64)
+        grouped_scalar = keep.tile([P, SCALAR_COEFFS, QUANT_ROWS * PACK], BF16, align_bytes=64)
         x_rows = x.rearrange("b (p j) n -> p b (j n)", j=PACK)
+        word_tiles = {}
         row_tiles = {}
 
         def load_chunk(half, chunk):
@@ -129,7 +130,8 @@ def tile_s2conv_pa_t_e_kernel(tc, x, psi_words, psi_scales, out):
             return raw
 
         def regroup_chunk(raw, chunk):
-            cols = slice(chunk * CHUNK_ROWS * PACK, (chunk + 1) * CHUNK_ROWS * PACK)
+            part = chunk % CHUNKS_PER_QUANT
+            cols = slice(part * CHUNK_ROWS * PACK, (part + 1) * CHUNK_ROWS * PACK)
             nc.vector.tensor_copy(
                 out=grouped_vector[:, :, cols].rearrange("p (c i) r -> p c r i", i=RUN),
                 in_=raw[:, :, 0:VECTOR_COEFFS].rearrange("p r (c i) -> p c r i", i=RUN),
@@ -139,17 +141,22 @@ def tile_s2conv_pa_t_e_kernel(tc, x, psi_words, psi_scales, out):
                 in_=raw[:, :, VECTOR_COEFFS:COEFFS].rearrange("p r (c i) -> p c r i", i=RUN),
             )
 
-        def quantise_half():
-            for first_n in reversed(range(0, COEFFS, QUANT_COEFFS)):
-                if first_n >= VECTOR_COEFFS:
-                    source = grouped_scalar[:, first_n - VECTOR_COEFFS :, :]
+        def quantise_rows(half, first_row):
+            if half not in word_tiles:
+                x_codes = words.tile([P, COEFFS, P], U32, align_bytes=64)
+                x_scales = words.tile([P, COEFFS, P], U8, align_bytes=64)
+                word_tiles[half] = (x_codes, x_scales)
+            x_codes, x_scales = word_tiles[half]
+            batch = slice(first_row, first_row + QUANT_ROWS)
+            for n in reversed(range(COEFFS)):
+                if n >= VECTOR_COEFFS:
+                    source = grouped_scalar[:, n - VECTOR_COEFFS, :]
                 else:
-                    source = grouped_vector[:, first_n:, :]
-                coeffs = slice(first_n, first_n + QUANT_COEFFS)
+                    source = grouped_vector[:, n, :]
                 nc.vector.quantize_mx(
-                    out=x_codes[:, coeffs, :].rearrange("p n b -> p (n b)").bitcast(FP8X4),
-                    scales=x_scales[:, coeffs, :].rearrange("p n b -> p (n b)"),
-                    in_=source[:, 0:QUANT_COEFFS, :].rearrange("p n r -> p (n r)"),
+                    out=x_codes[:, n, batch].bitcast(FP8X4),
+                    scales=x_scales[:, n, batch],
+                    in_=source,
                 )
 
         def multiply_bank(half, group, degree, first_u):
@@ -157,6 +164,7 @@ def tile_s2conv_pa_t_e_kernel(tc, x, psi_words, psi_scales, out):
                 rows = outs.tile([P, GROUP_FEATURES, ROW], F32)
                 row_tiles[(half, group)] = rows
             rows = row_tiles[(half, group)]
+            x_codes, x_scales = word_tiles[half]
             size = 2 * degree + 1
             first_n = degree * degree
             block = sum((2 * k + 1) ** 2 for k in range(degree))
@@ -210,7 +218,7 @@ def tile_s2conv_pa_t_e_kernel(tc, x, psi_words, psi_scales, out):
                         multiply_bank(step - 1, group, degree, first_u)
                 if step < HALVES:
                     regroup_chunk(raw, chunk)
+                    if (chunk + 1) % CHUNKS_PER_QUANT == 0:
+                        quantise_rows(step, (chunk + 1) * CHUNK_ROWS - QUANT_ROWS)
             if step > 0:
                 store_half(step - 1)
-            if step < HALVES:
-                quantise_half()

@@ -29,8 +29,8 @@ CHUNK_ROWS = 16
 CHUNKS = P // CHUNK_ROWS
 RAW_BUFFERS = 5
 
-SCALAR_COEFFS = COEFFS // 4
-VECTOR_COEFFS = COEFFS - SCALAR_COEFFS
+SCALAR_COEFFS = (28, 16)
+VECTOR_COEFFS = (COEFFS - SCALAR_COEFFS[0], COEFFS - SCALAR_COEFFS[1])
 RUN = 4
 QUANT_ROWS = 64
 CHUNKS_PER_QUANT = QUANT_ROWS // CHUNK_ROWS
@@ -52,20 +52,24 @@ def window(degree):
     return start, stop - start
 
 
-def banks_of_a_half():
+def banks_of_a_half(top_down):
     banks = []
     for group in range(GROUPS):
-        for degree in reversed(range(DEGREES)):
-            for first_u in reversed(range(0, 2 * degree + 1, PASSES_PER_BANK)):
-                banks.append((group, degree, first_u))
+        of_group = []
+        for degree in range(DEGREES):
+            for first_u in range(0, 2 * degree + 1, PASSES_PER_BANK):
+                of_group.append((group, degree, first_u))
+        if top_down:
+            of_group = list(reversed(of_group))
+        banks.extend(of_group)
     return banks
 
 
 def tile_s2conv_pa_t_e_kernel(tc, x, psi_words, psi_scales, out):
     nc = tc.nc
-    banks = banks_of_a_half()
-    banks_per_chunk = len(banks) // CHUNKS
-    assert banks_per_chunk * CHUNKS == len(banks)
+    banks_by_half = (banks_of_a_half(True), banks_of_a_half(True))
+    banks_per_chunk = len(banks_by_half[0]) // CHUNKS
+    assert banks_per_chunk * CHUNKS == len(banks_by_half[0])
 
     with ExitStack() as ctx:
         const = ctx.enter_context(tc.tile_pool(name="const", bufs=1))
@@ -114,8 +118,8 @@ def tile_s2conv_pa_t_e_kernel(tc, x, psi_words, psi_scales, out):
                 .rearrange("p (h g) w -> p h g w", g=GROUP_FEATURES),
             )
 
-        grouped_vector = keep.tile([P, VECTOR_COEFFS, QUANT_ROWS * PACK], BF16, align_bytes=64)
-        grouped_scalar = keep.tile([P, SCALAR_COEFFS, QUANT_ROWS * PACK], BF16, align_bytes=64)
+        grouped_vector = keep.tile([P, max(VECTOR_COEFFS), QUANT_ROWS * PACK], BF16, align_bytes=64)
+        grouped_scalar = keep.tile([P, max(SCALAR_COEFFS), QUANT_ROWS * PACK], BF16, align_bytes=64)
         x_rows = x.rearrange("b (p j) n -> p b (j n)", j=PACK)
         word_tiles = {}
         row_tiles = {}
@@ -129,16 +133,19 @@ def tile_s2conv_pa_t_e_kernel(tc, x, psi_words, psi_scales, out):
             )
             return raw
 
-        def regroup_chunk(raw, chunk):
+        def regroup_chunk(raw, half, chunk):
             part = chunk % CHUNKS_PER_QUANT
             cols = slice(part * CHUNK_ROWS * PACK, (part + 1) * CHUNK_ROWS * PACK)
+            split = SCALAR_COEFFS[half]
             nc.vector.tensor_copy(
-                out=grouped_vector[:, :, cols].rearrange("p (c i) r -> p c r i", i=RUN),
-                in_=raw[:, :, 0:VECTOR_COEFFS].rearrange("p r (c i) -> p c r i", i=RUN),
+                out=grouped_vector[:, 0 : COEFFS - split, cols].rearrange(
+                    "p (c i) r -> p c r i", i=RUN
+                ),
+                in_=raw[:, :, split:COEFFS].rearrange("p r (c i) -> p c r i", i=RUN),
             )
             nc.scalar.copy(
-                out=grouped_scalar[:, :, cols].rearrange("p (c i) r -> p c r i", i=RUN),
-                in_=raw[:, :, VECTOR_COEFFS:COEFFS].rearrange("p r (c i) -> p c r i", i=RUN),
+                out=grouped_scalar[:, 0:split, cols].rearrange("p (c i) r -> p c r i", i=RUN),
+                in_=raw[:, :, 0:split].rearrange("p r (c i) -> p c r i", i=RUN),
             )
 
         def quantise_rows(half, first_row):
@@ -148,11 +155,12 @@ def tile_s2conv_pa_t_e_kernel(tc, x, psi_words, psi_scales, out):
                 word_tiles[half] = (x_codes, x_scales)
             x_codes, x_scales = word_tiles[half]
             batch = slice(first_row, first_row + QUANT_ROWS)
+            split = SCALAR_COEFFS[half]
             for n in reversed(range(COEFFS)):
-                if n >= VECTOR_COEFFS:
-                    source = grouped_scalar[:, n - VECTOR_COEFFS, :]
+                if n < split:
+                    source = grouped_scalar[:, n, :]
                 else:
-                    source = grouped_vector[:, n, :]
+                    source = grouped_vector[:, n - split, :]
                 nc.vector.quantize_mx(
                     out=x_codes[:, n, batch].bitcast(FP8X4),
                     scales=x_scales[:, n, batch],
@@ -212,12 +220,12 @@ def tile_s2conv_pa_t_e_kernel(tc, x, psi_words, psi_scales, out):
                 if step < HALVES:
                     raw = load_chunk(step, chunk)
                 if step > 0:
-                    for group, degree, first_u in banks[
+                    for group, degree, first_u in banks_by_half[step - 1][
                         chunk * banks_per_chunk : (chunk + 1) * banks_per_chunk
                     ]:
                         multiply_bank(step - 1, group, degree, first_u)
                 if step < HALVES:
-                    regroup_chunk(raw, chunk)
+                    regroup_chunk(raw, step, chunk)
                     if (chunk + 1) % CHUNKS_PER_QUANT == 0:
                         quantise_rows(step, (chunk + 1) * CHUNK_ROWS - QUANT_ROWS)
             if step > 0:

@@ -29,7 +29,7 @@ CHUNK_ROWS = 16
 CHUNKS = P // CHUNK_ROWS
 RAW_BUFFERS = 5
 
-SCALAR_COEFFS = (28, 16)
+SCALAR_COEFFS = (32, 16)
 VECTOR_COEFFS = (COEFFS - SCALAR_COEFFS[0], COEFFS - SCALAR_COEFFS[1])
 RUN = 4
 QUANT_ROWS = 64
@@ -75,7 +75,7 @@ def tile_s2conv_pa_t_e_kernel(tc, x, psi_words, psi_scales, out):
         const = ctx.enter_context(tc.tile_pool(name="const", bufs=1))
         keep = ctx.enter_context(tc.tile_pool(name="keep", bufs=1))
         stream = ctx.enter_context(tc.tile_pool(name="stream", bufs=RAW_BUFFERS))
-        words = ctx.enter_context(tc.tile_pool(name="words", bufs=HALVES))
+        words = ctx.enter_context(tc.tile_pool(name="words", bufs=1))
         outs = ctx.enter_context(tc.tile_pool(name="outs", bufs=ROW_BUFFERS))
         psum = ctx.enter_context(tc.psum_pool(name="psum", bufs=PSUM_BANKS))
         ctx.enter_context(tc.manual_schedule())
@@ -118,10 +118,12 @@ def tile_s2conv_pa_t_e_kernel(tc, x, psi_words, psi_scales, out):
                 .rearrange("p (h g) w -> p h g w", g=GROUP_FEATURES),
             )
 
-        grouped_vector = keep.tile([P, max(VECTOR_COEFFS), QUANT_ROWS * PACK], BF16, align_bytes=64)
-        grouped_scalar = keep.tile([P, max(SCALAR_COEFFS), QUANT_ROWS * PACK], BF16, align_bytes=64)
+        grouped_even = keep.tile([P, COEFFS, QUANT_ROWS * PACK], BF16, align_bytes=64)
+        grouped_odd = keep.tile([P, COEFFS, QUANT_ROWS * PACK], BF16, align_bytes=64)
+        grouped = (grouped_even, grouped_odd)
+        x_codes = words.tile([P, COEFFS, P], U32, align_bytes=64)
+        x_scales = words.tile([P, COEFFS, P], U8, align_bytes=64)
         x_rows = x.rearrange("b (p j) n -> p b (j n)", j=PACK)
-        word_tiles = {}
         row_tiles = {}
 
         def load_chunk(half, chunk):
@@ -137,42 +139,31 @@ def tile_s2conv_pa_t_e_kernel(tc, x, psi_words, psi_scales, out):
             part = chunk % CHUNKS_PER_QUANT
             cols = slice(part * CHUNK_ROWS * PACK, (part + 1) * CHUNK_ROWS * PACK)
             split = SCALAR_COEFFS[half]
+            target = grouped[(chunk // CHUNKS_PER_QUANT) % 2]
             nc.vector.tensor_copy(
-                out=grouped_vector[:, 0 : COEFFS - split, cols].rearrange(
-                    "p (c i) r -> p c r i", i=RUN
-                ),
+                out=target[:, split:COEFFS, cols].rearrange("p (c i) r -> p c r i", i=RUN),
                 in_=raw[:, :, split:COEFFS].rearrange("p r (c i) -> p c r i", i=RUN),
             )
             nc.scalar.copy(
-                out=grouped_scalar[:, 0:split, cols].rearrange("p (c i) r -> p c r i", i=RUN),
+                out=target[:, 0:split, cols].rearrange("p (c i) r -> p c r i", i=RUN),
                 in_=raw[:, :, 0:split].rearrange("p r (c i) -> p c r i", i=RUN),
             )
 
-        def quantise_rows(half, first_row):
-            if half not in word_tiles:
-                x_codes = words.tile([P, COEFFS, P], U32, align_bytes=64)
-                x_scales = words.tile([P, COEFFS, P], U8, align_bytes=64)
-                word_tiles[half] = (x_codes, x_scales)
-            x_codes, x_scales = word_tiles[half]
-            batch = slice(first_row, first_row + QUANT_ROWS)
-            split = SCALAR_COEFFS[half]
+        def quantise_rows(quarters):
             for n in reversed(range(COEFFS)):
-                if n < split:
-                    source = grouped_scalar[:, n, :]
-                else:
-                    source = grouped_vector[:, n - split, :]
-                nc.vector.quantize_mx(
-                    out=x_codes[:, n, batch].bitcast(FP8X4),
-                    scales=x_scales[:, n, batch],
-                    in_=source,
-                )
+                for quarter in quarters:
+                    batch = slice(quarter * QUANT_ROWS, (quarter + 1) * QUANT_ROWS)
+                    nc.vector.quantize_mx(
+                        out=x_codes[:, n, batch].bitcast(FP8X4),
+                        scales=x_scales[:, n, batch],
+                        in_=grouped[quarter][:, n, :],
+                    )
 
         def multiply_bank(half, group, degree, first_u):
             if (half, group) not in row_tiles:
                 rows = outs.tile([P, GROUP_FEATURES, ROW], F32)
                 row_tiles[(half, group)] = rows
             rows = row_tiles[(half, group)]
-            x_codes, x_scales = word_tiles[half]
             size = 2 * degree + 1
             first_n = degree * degree
             block = sum((2 * k + 1) ** 2 for k in range(degree))
@@ -226,7 +217,9 @@ def tile_s2conv_pa_t_e_kernel(tc, x, psi_words, psi_scales, out):
                         multiply_bank(step - 1, group, degree, first_u)
                 if step < HALVES:
                     regroup_chunk(raw, step, chunk)
-                    if (chunk + 1) % CHUNKS_PER_QUANT == 0:
-                        quantise_rows(step, (chunk + 1) * CHUNK_ROWS - QUANT_ROWS)
+                    if step < HALVES - 1 and (chunk + 1) % CHUNKS_PER_QUANT == 0:
+                        quantise_rows((chunk // CHUNKS_PER_QUANT,))
+                    if step == HALVES - 1 and chunk == CHUNKS - 1:
+                        quantise_rows((0, 1))
             if step > 0:
                 store_half(step - 1)

@@ -29,7 +29,7 @@ CHUNK_ROWS = 16
 CHUNKS = P // CHUNK_ROWS
 RAW_BUFFERS = 5
 
-SCALAR_COEFFS = (32, 16)
+SCALAR_COEFFS = (32, 12)
 VECTOR_COEFFS = (COEFFS - SCALAR_COEFFS[0], COEFFS - SCALAR_COEFFS[1])
 RUN = 4
 QUANT_ROWS = 64
@@ -42,6 +42,8 @@ PASSES_PER_BANK = 4
 PSUM_BANKS = 8
 ROW_BUFFERS = 3
 STORE_FEATURES = 4
+BANKS_BY_CHUNK = (6, 6, 6, 6, 6, 5, 5, 0)
+HIGH_DEGREE = 5
 
 
 def window(degree):
@@ -52,24 +54,22 @@ def window(degree):
     return start, stop - start
 
 
-def banks_of_a_half(top_down):
+def block_start(degree):
+    return sum((2 * k + 1) ** 2 for k in range(degree))
+
+
+def banks_of_degrees(group, degrees):
     banks = []
-    for group in range(GROUPS):
-        of_group = []
-        for degree in range(DEGREES):
-            for first_u in range(0, 2 * degree + 1, PASSES_PER_BANK):
-                of_group.append((group, degree, first_u))
-        if top_down:
-            of_group = list(reversed(of_group))
-        banks.extend(of_group)
-    return banks
+    for degree in degrees:
+        for first_u in range(0, 2 * degree + 1, PASSES_PER_BANK):
+            banks.append((group, degree, first_u))
+    return list(reversed(banks))
 
 
 def tile_s2conv_pa_t_e_kernel(tc, x, psi_words, psi_scales, out):
     nc = tc.nc
-    banks_by_half = (banks_of_a_half(True), banks_of_a_half(True))
-    banks_per_chunk = len(banks_by_half[0]) // CHUNKS
-    assert banks_per_chunk * CHUNKS == len(banks_by_half[0])
+    first_banks = [bank for group in range(GROUPS) for bank in banks_of_degrees(group, range(DEGREES))]
+    assert sum(BANKS_BY_CHUNK) == len(first_banks)
 
     with ExitStack() as ctx:
         const = ctx.enter_context(tc.tile_pool(name="const", bufs=1))
@@ -124,7 +124,6 @@ def tile_s2conv_pa_t_e_kernel(tc, x, psi_words, psi_scales, out):
         x_codes = words.tile([P, COEFFS, P], U32, align_bytes=64)
         x_scales = words.tile([P, COEFFS, P], U8, align_bytes=64)
         x_rows = x.rearrange("b (p j) n -> p b (j n)", j=PACK)
-        row_tiles = {}
 
         def load_chunk(half, chunk):
             first_row = half * P + chunk * CHUNK_ROWS
@@ -159,19 +158,11 @@ def tile_s2conv_pa_t_e_kernel(tc, x, psi_words, psi_scales, out):
                         in_=grouped[quarter][:, n, :],
                     )
 
-        def multiply_bank(half, group, degree, first_u):
-            if (half, group) not in row_tiles:
-                rows = outs.tile([P, GROUP_FEATURES, ROW], F32)
-                row_tiles[(half, group)] = rows
-            rows = row_tiles[(half, group)]
-            size = 2 * degree + 1
-            first_n = degree * degree
-            block = sum((2 * k + 1) ** 2 for k in range(degree))
-            start, width = window(degree)
-            count = min(PASSES_PER_BANK, size - first_u)
+        def multiply_bank(group, degree, first_u, most=PASSES_PER_BANK):
+            count = min(most, 2 * degree + 1 - first_u)
             bank = psum.tile([P, PASSES_PER_BANK, PASS_COLS], F32)
             for k in range(count):
-                n = first_n + first_u + k
+                n = degree * degree + first_u + k
                 nc.tensor.matmul_mx(
                     out=bank[:, k, :],
                     lhsT=x_codes[:, n, :].bitcast(FP8X4),
@@ -181,45 +172,87 @@ def tile_s2conv_pa_t_e_kernel(tc, x, psi_words, psi_scales, out):
                     start=True,
                     stop=True,
                 )
-            skip = first_n - start
+            start, width = window(degree)
+            skip = degree * degree - start
             products = bank[:, 0:count, 0 : GROUP_FEATURES * width].rearrange(
                 "p k (g w) -> p g k w", w=width
             )
-            place = block + first_u * size
-            nc.scalar.mul(
-                out=rows[:, :, place : place + count * size].rearrange(
-                    "p g (k m) -> p g k m", m=size
-                ),
-                in_=products[:, :, :, skip : skip + size],
-                mul=SCALE,
+            return products[:, :, :, skip : skip + 2 * degree + 1]
+
+        def scale_into(rows, place, products, on_vector=False):
+            count, size = products.shape[2], products.shape[3]
+            into = rows[:, :, place : place + count * size].rearrange("p g (k m) -> p g k m", m=size)
+            if on_vector:
+                nc.vector.tensor_scalar_mul(into, products, SCALE)
+            else:
+                nc.scalar.mul(out=into, in_=products, mul=SCALE)
+
+        def store(rows, columns, half, first_g):
+            features = slice(first_g, first_g + rows.shape[1])
+            nc.sync.dma_start(
+                out=out[features, half * P : (half + 1) * P, columns].rearrange("g b c -> b g c"),
+                in_=rows,
             )
 
-        def store_half(half):
-            for group in range(GROUPS):
-                rows = row_tiles[(half, group)]
-                for first_g in range(0, GROUP_FEATURES, STORE_FEATURES):
-                    g = group * GROUP_FEATURES + first_g
-                    nc.sync.dma_start(
-                        out=out[g : g + STORE_FEATURES, half * P : (half + 1) * P, :].rearrange(
-                            "g b c -> b g c"
-                        ),
-                        in_=rows[:, first_g : first_g + STORE_FEATURES, :],
-                    )
-
-        for step in range(HALVES + 1):
-            for chunk in range(CHUNKS):
-                if step < HALVES:
-                    raw = load_chunk(step, chunk)
-                if step > 0:
-                    for group, degree, first_u in banks_by_half[step - 1][
-                        chunk * banks_per_chunk : (chunk + 1) * banks_per_chunk
-                    ]:
-                        multiply_bank(step - 1, group, degree, first_u)
-                if step < HALVES:
-                    regroup_chunk(raw, step, chunk)
-                    if step < HALVES - 1 and (chunk + 1) % CHUNKS_PER_QUANT == 0:
-                        quantise_rows((chunk // CHUNKS_PER_QUANT,))
-                    if step == HALVES - 1 and chunk == CHUNKS - 1:
-                        quantise_rows((0, 1))
-            if step > 0:
-                store_half(step - 1)
+        for chunk in range(CHUNKS):
+            raw = load_chunk(0, chunk)
+            regroup_chunk(raw, 0, chunk)
+            if (chunk + 1) % CHUNKS_PER_QUANT == 0:
+                quantise_rows((chunk // CHUNKS_PER_QUANT,))
+        whole_rows = {}
+        for chunk in range(CHUNKS):
+            raw = load_chunk(1, chunk)
+            done = sum(BANKS_BY_CHUNK[:chunk])
+            for group, degree, first_u in first_banks[done : done + BANKS_BY_CHUNK[chunk]]:
+                if group not in whole_rows:
+                    rows = outs.tile([P, GROUP_FEATURES, ROW], F32)
+                    whole_rows[group] = rows
+                place = block_start(degree) + first_u * (2 * degree + 1)
+                scale_into(
+                    whole_rows[group], place, multiply_bank(group, degree, first_u)
+                )
+            regroup_chunk(raw, 1, chunk)
+        for group in range(GROUPS):
+            for first in range(0, GROUP_FEATURES, STORE_FEATURES):
+                store(
+                    whole_rows[group][:, first : first + STORE_FEATURES, :],
+                    slice(0, ROW),
+                    0,
+                    group * GROUP_FEATURES + first,
+                )
+        quantise_rows((0, 1))
+        high = range(HIGH_DEGREE, DEGREES)
+        low = range(HIGH_DEGREE)
+        cut = block_start(HIGH_DEGREE)
+        cut += -cut % 8
+        for group in range(GROUPS):
+            rows = outs.tile([P, GROUP_FEATURES, ROW - cut], F32)
+            for bank_group, degree, first_u in banks_of_degrees(group, high):
+                place = block_start(degree) + first_u * (2 * degree + 1) - cut
+                products = multiply_bank(bank_group, degree, first_u)
+                if place < 0:
+                    scale_into(rows, 0, products[:, :, 0:1, -place:])
+                    place += 2 * degree + 1
+                    products = products[:, :, 1:, :]
+                scale_into(rows, place, products)
+            store(rows[:], slice(cut, ROW), 1, group * GROUP_FEATURES)
+        low_rows = outs.tile([P, OUT_FEATURES, cut], F32, tag="rows")
+        below = cut - block_start(HIGH_DEGREE)
+        low_banks = [banks_of_degrees(group, low) for group in range(GROUPS)]
+        for group in range(GROUPS):
+            features = slice(group * GROUP_FEATURES, (group + 1) * GROUP_FEATURES)
+            products = multiply_bank(group, HIGH_DEGREE, 0, 1)[:, :, :, 0:below]
+            scale_into(low_rows[:, features], cut - below, products, on_vector=group == 1)
+        for pair in zip(*low_banks):
+            for group, degree, first_u in pair:
+                features = slice(group * GROUP_FEATURES, (group + 1) * GROUP_FEATURES)
+                place = block_start(degree) + first_u * (2 * degree + 1)
+                scale_into(
+                    low_rows[:, features],
+                    place,
+                    multiply_bank(group, degree, first_u),
+                    on_vector=group == 1,
+                )
+        for group in range(GROUPS):
+            features = slice(group * GROUP_FEATURES, (group + 1) * GROUP_FEATURES)
+            store(low_rows[:, features], slice(0, cut), 1, group * GROUP_FEATURES)

@@ -44,6 +44,8 @@ ROW_BUFFERS = 3
 STORE_FEATURES = 4
 BANKS_BY_CHUNK = (6, 6, 6, 6, 6, 5, 5, 0)
 HIGH_DEGREE = 5
+HIGH_PLANE = 24
+DEFERRED = range(CHUNKS - RAW_BUFFERS, CHUNKS)
 
 
 def window(degree):
@@ -134,22 +136,17 @@ def tile_s2conv_pa_t_e_kernel(tc, x, psi_words, psi_scales, out):
             )
             return raw
 
-        def regroup_chunk(raw, half, chunk):
+        def regroup(engine_copy, raw, chunk, first, beyond):
             part = chunk % CHUNKS_PER_QUANT
             cols = slice(part * CHUNK_ROWS * PACK, (part + 1) * CHUNK_ROWS * PACK)
-            split = SCALAR_COEFFS[half]
-            target = grouped[(chunk // CHUNKS_PER_QUANT) % 2]
-            nc.vector.tensor_copy(
-                out=target[:, split:COEFFS, cols].rearrange("p (c i) r -> p c r i", i=RUN),
-                in_=raw[:, :, split:COEFFS].rearrange("p r (c i) -> p c r i", i=RUN),
-            )
-            nc.scalar.copy(
-                out=target[:, 0:split, cols].rearrange("p (c i) r -> p c r i", i=RUN),
-                in_=raw[:, :, 0:split].rearrange("p r (c i) -> p c r i", i=RUN),
+            target = grouped[chunk // CHUNKS_PER_QUANT]
+            engine_copy(
+                out=target[:, first:beyond, cols].rearrange("p (c i) r -> p c r i", i=RUN),
+                in_=raw[:, :, first:beyond].rearrange("p r (c i) -> p c r i", i=RUN),
             )
 
-        def quantise_rows(quarters):
-            for n in reversed(range(COEFFS)):
+        def quantise_rows(quarters, coeffs=range(COEFFS)):
+            for n in reversed(coeffs):
                 for quarter in quarters:
                     batch = slice(quarter * QUANT_ROWS, (quarter + 1) * QUANT_ROWS)
                     nc.vector.quantize_mx(
@@ -196,10 +193,12 @@ def tile_s2conv_pa_t_e_kernel(tc, x, psi_words, psi_scales, out):
 
         for chunk in range(CHUNKS):
             raw = load_chunk(0, chunk)
-            regroup_chunk(raw, 0, chunk)
+            regroup(nc.vector.tensor_copy, raw, chunk, SCALAR_COEFFS[0], COEFFS)
+            regroup(nc.scalar.copy, raw, chunk, 0, SCALAR_COEFFS[0])
             if (chunk + 1) % CHUNKS_PER_QUANT == 0:
                 quantise_rows((chunk // CHUNKS_PER_QUANT,))
         whole_rows = {}
+        last_raws = []
         for chunk in range(CHUNKS):
             raw = load_chunk(1, chunk)
             done = sum(BANKS_BY_CHUNK[:chunk])
@@ -211,7 +210,10 @@ def tile_s2conv_pa_t_e_kernel(tc, x, psi_words, psi_scales, out):
                 scale_into(
                     whole_rows[group], place, multiply_bank(group, degree, first_u)
                 )
-            regroup_chunk(raw, 1, chunk)
+            high_first = HIGH_PLANE if chunk in DEFERRED else SCALAR_COEFFS[1]
+            regroup(nc.vector.tensor_copy, raw, chunk, high_first, COEFFS)
+            regroup(nc.scalar.copy, raw, chunk, 0, SCALAR_COEFFS[1])
+            last_raws.append(raw)
         for group in range(GROUPS):
             for first in range(0, GROUP_FEATURES, STORE_FEATURES):
                 store(
@@ -220,7 +222,10 @@ def tile_s2conv_pa_t_e_kernel(tc, x, psi_words, psi_scales, out):
                     0,
                     group * GROUP_FEATURES + first,
                 )
-        quantise_rows((0, 1))
+        quantise_rows((0, 1), range(HIGH_DEGREE * HIGH_DEGREE, COEFFS))
+        for chunk in DEFERRED:
+            regroup(nc.vector.tensor_copy, last_raws[chunk], chunk, SCALAR_COEFFS[1], HIGH_PLANE)
+        quantise_rows((0, 1), range(HIGH_DEGREE * HIGH_DEGREE))
         high = range(HIGH_DEGREE, DEGREES)
         low = range(HIGH_DEGREE)
         cut = block_start(HIGH_DEGREE)

@@ -27,7 +27,9 @@ FLOPS = 2 * FEATURES * BATCH * OUT_FEATURES * ROW
 HALVES = BATCH // P
 CHUNK_ROWS = 16
 CHUNKS = P // CHUNK_ROWS
-RAW_BUFFERS = 5
+BUFFER_CHUNKS = 2
+RAW_BUFFERS = 3
+PAIR_LOADS = {(1, 0), (1, 2), (1, 4)}
 
 SCALAR_COEFFS = (32, 12)
 VECTOR_COEFFS = (COEFFS - SCALAR_COEFFS[0], COEFFS - SCALAR_COEFFS[1])
@@ -41,11 +43,11 @@ GROUPS = OUT_FEATURES // GROUP_FEATURES
 PASSES_PER_BANK = 4
 PSUM_BANKS = 8
 ROW_BUFFERS = 3
-STORE_FEATURES = 4
+STORE_FEATURES = 8
 BANKS_BY_CHUNK = (6, 6, 6, 6, 6, 5, 5, 0)
 HIGH_DEGREE = 5
 HIGH_PLANE = 24
-DEFERRED = range(CHUNKS - RAW_BUFFERS, CHUNKS)
+DEFERRED = range(CHUNKS - RAW_BUFFERS * BUFFER_CHUNKS, CHUNKS)
 
 
 def window(degree):
@@ -126,15 +128,26 @@ def tile_s2conv_pa_t_e_kernel(tc, x, psi_words, psi_scales, out):
         x_codes = words.tile([P, COEFFS, P], U32, align_bytes=64)
         x_scales = words.tile([P, COEFFS, P], U8, align_bytes=64)
         x_rows = x.rearrange("b (p j) n -> p b (j n)", j=PACK)
+        buffers = []
 
         def load_chunk(half, chunk):
+            part = chunk % BUFFER_CHUNKS
+            if part == 0:
+                buffer = stream.tile([P, BUFFER_CHUNKS * CHUNK_ROWS * PACK, COEFFS], BF16)
+                buffers.append(buffer)
+            rows = 0
+            if (half, chunk) in PAIR_LOADS:
+                rows = BUFFER_CHUNKS * CHUNK_ROWS
+            elif (half, chunk - part) not in PAIR_LOADS:
+                rows = CHUNK_ROWS
+            cols = slice(part * CHUNK_ROWS * PACK, part * CHUNK_ROWS * PACK + rows * PACK)
             first_row = half * P + chunk * CHUNK_ROWS
-            raw = stream.tile([P, CHUNK_ROWS * PACK, COEFFS], BF16)
-            nc.sync.dma_start(
-                out=raw[:].rearrange("p (b j) n -> p b (j n)", j=PACK),
-                in_=x_rows[:, first_row : first_row + CHUNK_ROWS, :],
-            )
-            return raw
+            if rows > 0:
+                nc.sync.dma_start(
+                    out=buffers[-1][:, cols, :].rearrange("p (b j) n -> p b (j n)", j=PACK),
+                    in_=x_rows[:, first_row : first_row + rows, :],
+                )
+            return buffers[-1][:, part * CHUNK_ROWS * PACK : (part + 1) * CHUNK_ROWS * PACK, :]
 
         def regroup(engine_copy, raw, chunk, first, beyond):
             part = chunk % CHUNKS_PER_QUANT

from contextlib import ExitStack
import math

import concourse.mybir as mybir

BF16 = mybir.dt.bfloat16
F32 = mybir.dt.float32
I32 = mybir.dt.int32
U32 = mybir.dt.uint32
U8 = mybir.dt.uint8
FP8X4 = mybir.dt.float8_e4m3fn_x4

P = 128
PACK = 4
BATCH = 256
FEATURES = P * PACK
COEFFS = 64
DEGREES = 8
OUT_FEATURES = 16
ROW = 680
SCALE = 1.0 / math.sqrt(FEATURES)

assert ROW == sum((2 * degree + 1) ** 2 for degree in range(DEGREES))

FLOPS = 2 * FEATURES * BATCH * OUT_FEATURES * ROW

HALVES = BATCH // P
CHUNK_ROWS = 16
CHUNKS = P // CHUNK_ROWS
BUFFER_CHUNKS = 2
RAW_BUFFERS = 3
PAIR_LOADS = {(1, 0), (1, 2), (1, 4)}

SCALAR_COEFFS = (32, 12)
VECTOR_COEFFS = (COEFFS - SCALAR_COEFFS[0], COEFFS - SCALAR_COEFFS[1])
RUN = 4
QUANT_ROWS = 64
CHUNKS_PER_QUANT = QUANT_ROWS // CHUNK_ROWS

PASS_COLS = 128
GROUP_FEATURES = 8
GROUPS = OUT_FEATURES // GROUP_FEATURES
PASSES_PER_BANK = 4
PSUM_BANKS = 8
ROW_BUFFERS = 3
STORE_FEATURES = 8
BANKS_BY_CHUNK = (6, 6, 6, 6, 6, 5, 5, 0)
HIGH_DEGREE = 5
HIGH_PLANE = 24
DEFERRED = range(CHUNKS - RAW_BUFFERS * BUFFER_CHUNKS, CHUNKS)


def window(degree):
    first = degree * degree
    beyond = first + 2 * degree + 1
    start = first - first % PACK
    stop = beyond + (-beyond) % PACK
    return start, stop - start


def block_start(degree):
    return sum((2 * k + 1) ** 2 for k in range(degree))


def banks_of_degrees(group, degrees):
    banks = []
    for degree in degrees:
        for first_u in range(0, 2 * degree + 1, PASSES_PER_BANK):
            banks.append((group, degree, first_u))
    return list(reversed(banks))


def tile_s2conv_pa_t_e_kernel(tc, x, psi_words, psi_scales, out):
    nc = tc.nc
    first_banks = [bank for group in range(GROUPS) for bank in banks_of_degrees(group, range(DEGREES))]
    assert sum(BANKS_BY_CHUNK) == len(first_banks)

    with ExitStack() as ctx:
        const = ctx.enter_context(tc.tile_pool(name="const", bufs=1))
        keep = ctx.enter_context(tc.tile_pool(name="keep", bufs=1))
        stream = ctx.enter_context(tc.tile_pool(name="stream", bufs=RAW_BUFFERS))
        words = ctx.enter_context(tc.tile_pool(name="words", bufs=1))
        outs = ctx.enter_context(tc.tile_pool(name="outs", bufs=ROW_BUFFERS))
        psum = ctx.enter_context(tc.psum_pool(name="psum", bufs=PSUM_BANKS))
        ctx.enter_context(tc.manual_schedule())

        psi_raw = const.tile([P, OUT_FEATURES, COEFFS], U32)
        nc.sync.dma_start(
            out=psi_raw[:].bitcast(I32),
            in_=psi_words.rearrange("g p n t -> p g (n t)").bitcast(I32),
        )
        scale_raw = const.tile([P, OUT_FEATURES, COEFFS], U8)
        nc.vector.memset(scale_raw[:].bitcast(I32), 0)
        for quadrant in range(4):
            nc.sync.dma_start(
                out=scale_raw[32 * quadrant : 32 * quadrant + 4, :, :].bitcast(I32),
                in_=psi_scales[:, 4 * quadrant : 4 * quadrant + 4, :]
                .rearrange("g r n -> r g n")
                .bitcast(I32),
            )
        filter_codes = const.tile([P, DEGREES, GROUPS, PASS_COLS], U32, align_bytes=64)
        filter_scales = const.tile([P, DEGREES, GROUPS, PASS_COLS], U8, align_bytes=64)
        nc.vector.memset(filter_codes[:].bitcast(I32), 0)
        nc.vector.memset(filter_scales[:].bitcast(I32), 0)
        for degree in range(DEGREES):
            start, width = window(degree)
            used = GROUP_FEATURES * width
            nc.vector.tensor_copy(
                out=filter_codes[:, degree, :, 0:used]
                .bitcast(I32)
                .rearrange("p h (g w) -> p h g w", w=width),
                in_=psi_raw[:, :, start : start + width]
                .bitcast(I32)
                .rearrange("p (h g) w -> p h g w", g=GROUP_FEATURES),
            )
            nc.vector.tensor_copy(
                out=filter_scales[:, degree, :, 0:used]
                .bitcast(I32)
                .rearrange("p h (g w) -> p h g w", w=width // 4),
                in_=scale_raw[:, :, start : start + width]
                .bitcast(I32)
                .rearrange("p (h g) w -> p h g w", g=GROUP_FEATURES),
            )

        grouped_even = keep.tile([P, COEFFS, QUANT_ROWS * PACK], BF16, align_bytes=64)
        grouped_odd = keep.tile([P, COEFFS, QUANT_ROWS * PACK], BF16, align_bytes=64)
        grouped = (grouped_even, grouped_odd)
        x_codes = words.tile([P, COEFFS, P], U32, align_bytes=64)
        x_scales = words.tile([P, COEFFS, P], U8, align_bytes=64)
        x_rows = x.rearrange("b (p j) n -> p b (j n)", j=PACK)
        buffers = []

        def load_chunk(half, chunk):
            part = chunk % BUFFER_CHUNKS
            if part == 0:
                buffer = stream.tile([P, BUFFER_CHUNKS * CHUNK_ROWS * PACK, COEFFS], BF16)
                buffers.append(buffer)
            rows = 0
            if (half, chunk) in PAIR_LOADS:
                rows = BUFFER_CHUNKS * CHUNK_ROWS
            elif (half, chunk - part) not in PAIR_LOADS:
                rows = CHUNK_ROWS
            cols = slice(part * CHUNK_ROWS * PACK, part * CHUNK_ROWS * PACK + rows * PACK)
            first_row = half * P + chunk * CHUNK_ROWS
            if rows > 0:
                nc.sync.dma_start(
                    out=buffers[-1][:, cols, :].rearrange("p (b j) n -> p b (j n)", j=PACK),
                    in_=x_rows[:, first_row : first_row + rows, :],
                )
            return buffers[-1][:, part * CHUNK_ROWS * PACK : (part + 1) * CHUNK_ROWS * PACK, :]

        def regroup(engine_copy, raw, chunk, first, beyond):
            part = chunk % CHUNKS_PER_QUANT
            cols = slice(part * CHUNK_ROWS * PACK, (part + 1) * CHUNK_ROWS * PACK)
            target = grouped[chunk // CHUNKS_PER_QUANT]
            engine_copy(
                out=target[:, first:beyond, cols].rearrange("p (c i) r -> p c r i", i=RUN),
                in_=raw[:, :, first:beyond].rearrange("p r (c i) -> p c r i", i=RUN),
            )

        def quantise_rows(quarters, coeffs=range(COEFFS)):
            for n in reversed(coeffs):
                for quarter in quarters:
                    batch = slice(quarter * QUANT_ROWS, (quarter + 1) * QUANT_ROWS)
                    nc.vector.quantize_mx(
                        out=x_codes[:, n, batch].bitcast(FP8X4),
                        scales=x_scales[:, n, batch],
                        in_=grouped[quarter][:, n, :],
                    )

        def multiply_bank(group, degree, first_u, most=PASSES_PER_BANK):
            count = min(most, 2 * degree + 1 - first_u)
            bank = psum.tile([P, PASSES_PER_BANK, PASS_COLS], F32)
            for k in range(count):
                n = degree * degree + first_u + k
                nc.tensor.matmul_mx(
                    out=bank[:, k, :],
                    lhsT=x_codes[:, n, :].bitcast(FP8X4),
                    lhsT_scale=x_scales[:, n, :],
                    rhs=filter_codes[:, degree, group, :].bitcast(FP8X4),
                    rhs_scale=filter_scales[:, degree, group, :],
                    start=True,
                    stop=True,
                )
            start, width = window(degree)
            skip = degree * degree - start
            products = bank[:, 0:count, 0 : GROUP_FEATURES * width].rearrange(
                "p k (g w) -> p g k w", w=width
            )
            return products[:, :, :, skip : skip + 2 * degree + 1]

        def scale_into(rows, place, products, on_vector=False):
            count, size = products.shape[2], products.shape[3]
            into = rows[:, :, place : place + count * size].rearrange("p g (k m) -> p g k m", m=size)
            if on_vector:
                nc.vector.tensor_scalar_mul(into, products, SCALE)
            else:
                nc.scalar.mul(out=into, in_=products, mul=SCALE)

        def store(rows, columns, half, first_g):
            features = slice(first_g, first_g + rows.shape[1])
            nc.sync.dma_start(
                out=out[features, half * P : (half + 1) * P, columns].rearrange("g b c -> b g c"),
                in_=rows,
            )

        for chunk in range(CHUNKS):
            raw = load_chunk(0, chunk)
            regroup(nc.vector.tensor_copy, raw, chunk, SCALAR_COEFFS[0], COEFFS)
            regroup(nc.scalar.copy, raw, chunk, 0, SCALAR_COEFFS[0])
            if (chunk + 1) % CHUNKS_PER_QUANT == 0:
                quantise_rows((chunk // CHUNKS_PER_QUANT,))
        whole_rows = {}
        last_raws = []
        for chunk in range(CHUNKS):
            raw = load_chunk(1, chunk)
            done = sum(BANKS_BY_CHUNK[:chunk])
            for group, degree, first_u in first_banks[done : done + BANKS_BY_CHUNK[chunk]]:
                if group not in whole_rows:
                    rows = outs.tile([P, GROUP_FEATURES, ROW], F32)
                    whole_rows[group] = rows
                place = block_start(degree) + first_u * (2 * degree + 1)
                scale_into(
                    whole_rows[group], place, multiply_bank(group, degree, first_u)
                )
            high_first = HIGH_PLANE if chunk in DEFERRED else SCALAR_COEFFS[1]
            regroup(nc.vector.tensor_copy, raw, chunk, high_first, COEFFS)
            regroup(nc.scalar.copy, raw, chunk, 0, SCALAR_COEFFS[1])
            last_raws.append(raw)
        for group in range(GROUPS):
            for first in range(0, GROUP_FEATURES, STORE_FEATURES):
                store(
                    whole_rows[group][:, first : first + STORE_FEATURES, :],
                    slice(0, ROW),
                    0,
                    group * GROUP_FEATURES + first,
                )
        quantise_rows((0, 1), range(HIGH_DEGREE * HIGH_DEGREE, COEFFS))
        for chunk in DEFERRED:
            regroup(nc.vector.tensor_copy, last_raws[chunk], chunk, SCALAR_COEFFS[1], HIGH_PLANE)
        quantise_rows((0, 1), range(HIGH_DEGREE * HIGH_DEGREE))
        high = range(HIGH_DEGREE, DEGREES)
        low = range(HIGH_DEGREE)
        cut = block_start(HIGH_DEGREE)
        cut += -cut % 8
        for group in range(GROUPS):
            rows = outs.tile([P, GROUP_FEATURES, ROW - cut], F32)
            for bank_group, degree, first_u in banks_of_degrees(group, high):
                place = block_start(degree) + first_u * (2 * degree + 1) - cut
                products = multiply_bank(bank_group, degree, first_u)
                if place < 0:
                    scale_into(rows, 0, products[:, :, 0:1, -place:])
                    place += 2 * degree + 1
                    products = products[:, :, 1:, :]
                scale_into(rows, place, products)
            store(rows[:], slice(cut, ROW), 1, group * GROUP_FEATURES)
        low_rows = outs.tile([P, OUT_FEATURES, cut], F32, tag="rows")
        below = cut - block_start(HIGH_DEGREE)
        low_banks = [banks_of_degrees(group, low) for group in range(GROUPS)]
        for group in range(GROUPS):
            features = slice(group * GROUP_FEATURES, (group + 1) * GROUP_FEATURES)
            products = multiply_bank(group, HIGH_DEGREE, 0, 1)[:, :, :, 0:below]
            scale_into(low_rows[:, features], cut - below, products, on_vector=group == 1)
        for pair in zip(*low_banks):
            for group, degree, first_u in pair:
                features = slice(group * GROUP_FEATURES, (group + 1) * GROUP_FEATURES)
                place = block_start(degree) + first_u * (2 * degree + 1)
                scale_into(
                    low_rows[:, features],
                    place,
                    multiply_bank(group, degree, first_u),
                    on_vector=group == 1,
                )
        for group in range(GROUPS):
            features = slice(group * GROUP_FEATURES, (group + 1) * GROUP_FEATURES)
            store(low_rows[:, features], slice(0, cut), 1, group * GROUP_FEATURES)
